import numpy as np
import ml_dtypes

BF16 = ml_dtypes.bfloat16


def bf(x):
    return np.asarray(x, np.float32).astype(BF16)


def f32(x):
    return np.asarray(x, np.float32)


def f64(x):
    return np.asarray(x).astype(np.float64)


def striped(idx):
    return np.tile(idx.reshape(-1, 16).T, (8, 1))


B, S, N, K, Q, H = 1024, 512, 128, 256, 128, 512


def setup_inputs():
    return {
        "base": f32(np.random.standard_normal((B, S))),
        "xt": f32(np.random.standard_normal((B, N))),
        "xid": bf(np.random.standard_normal((K, B))),
        "cond": bf(np.random.standard_normal((Q, B))),
        "w1": bf(np.random.standard_normal((K + Q, H)) / np.sqrt(K + Q)),
        "b1": f32(0.1 * np.random.standard_normal((H, 1))),
        "w3": bf(0.7 * np.random.standard_normal((H, N + N)) / np.sqrt(H)),
        "offs": striped(np.random.permutation(S)[:N]),
    }


def reference(base, xt, xid, cond, w1, b1, w3, offs):
    idx = offs[:16].T.reshape(-1)
    u = np.concatenate([f64(xid), f64(cond)], axis=0)
    hid = np.maximum(f64(w1).T @ u + f64(b1), 0.0)
    st = hid.T @ f64(w3)
    res = f64(base).copy()
    res[:, idx] = f64(xt) * np.exp(st[:, :N]) + st[:, N:]
    return res

@@ -1,0 +1,79 @@
+import concourse.mybir as mybir
+
+F32, BF16, U16 = mybir.dt.float32, mybir.dt.bfloat16, mybir.dt.uint16
+ACT = mybir.ActivationFunctionType
+ALU = mybir.AluOpType
+
+P = 128
+B, S, N = 1024, 512, 128
+K, H = 384, 512
+KB, HB, RB = K // P, H // P, B // P
+CHUNK = 512
+FLOPS = 2 * B * (K * H + H * 2 * N)
+
+
+def tile_affine_coupling_layer_s_kernel(tc, base, xt, xid, cond, w1, b1, w3, offs, out):
+    nc = tc.nc
+    with (
+        tc.tile_pool(name="held", bufs=1) as held,
+        tc.tile_pool(name="hidden", bufs=2) as hidden,
+        tc.tile_pool(name="work", bufs=3) as work,
+        tc.psum_pool(name="psum_hid", bufs=4) as psum_hid,
+        tc.psum_pool(name="psum_st", bufs=4) as psum_st,
+    ):
+        offsets = held.tile([P, N // 16], U16, name="offsets")
+        nc.sync.dma_start(offsets[:], offs)
+
+        w1_sb = [held.tile([P, H], BF16, name=f"w1_sb{kb}") for kb in range(KB)]
+        u_sb = [held.tile([P, B], BF16, name=f"u_sb{kb}") for kb in range(KB)]
+        u_rows = [xid[0:P, :], xid[P : 2 * P, :], cond]
+        for kb in range(KB):
+            nc.sync.dma_start(w1_sb[kb][:], w1[kb * P : (kb + 1) * P, :])
+            nc.scalar.dma_start(u_sb[kb][:], u_rows[kb])
+
+        b1_sb = held.tile([P, HB], F32, name="b1_sb")
+        with nc.allow_non_contiguous_dma(reason="512 biases, one to a partition and block"):
+            nc.scalar.dma_start(b1_sb[:], b1.rearrange("(hb p) o -> p (hb o)", p=P))
+        w3_sb = held.tile([P, HB, 2 * N], BF16, name="w3_sb")
+        nc.sync.dma_start(w3_sb[:], w3.rearrange("(hb p) j -> p hb j", p=P))
+        xt_sb = held.tile([P, RB, N], F32, name="xt_sb")
+        nc.scalar.dma_start(xt_sb[:], xt.rearrange("(rb p) j -> p rb j", p=P))
+
+        window = [held.tile([P, S], F32, name=f"window{rb}") for rb in range(RB)]
+        for rb in range(RB):
+            queue = nc.sync if rb % 2 == 0 else nc.scalar
+            queue.dma_start(window[rb][:], base[rb * P : (rb + 1) * P, :])
+
+        for c in range(B // CHUNK):
+            hid = hidden.tile([P, HB, CHUNK], BF16, name="hid")
+            for hb in range(HB):
+                acc = psum_hid.tile([P, CHUNK], F32, name="acc")
+                for kb in range(KB):
+                    nc.tensor.matmul(
+                        acc[:],
+                        w1_sb[kb][:, hb * P : (hb + 1) * P],
+                        u_sb[kb][:, c * CHUNK : (c + 1) * CHUNK],
+                        start=(kb == 0),
+                        stop=(kb == KB - 1),
+                    )
+                nc.scalar.activation(hid[:, hb, :], acc[:], ACT.Relu, bias=b1_sb[:, hb : hb + 1])
+
+            for i in range(CHUNK // P):
+                rb = c * (CHUNK // P) + i
+                st = psum_st.tile([P, 2 * N], F32, name="st")
+                for hb in range(HB):
+                    nc.tensor.matmul(
+                        st[:],
+                        hid[:, hb, i * P : (i + 1) * P],
+                        w3_sb[:, hb, :],
+                        start=(hb == 0),
+                        stop=(hb == HB - 1),
+                    )
+                scale = work.tile([P, N], F32, name="scale")
+                nc.scalar.activation(scale[:], st[:, 0:N], ACT.Exp)
+                shift = work.tile([P, N], F32, name="shift")
+                nc.scalar.activation(shift[:], st[:, N : 2 * N], ACT.Copy)
+                product = work.tile([P, N], F32, name="product")
+                nc.vector.tensor_tensor(product[:], xt_sb[:, rb, :], scale[:], ALU.mult)
+                nc.vector.tensor_tensor(window[rb][:].indirect(offsets[:]), product[:], shift[:], ALU.add)
+                nc.sync.dma_start(out[rb * P : (rb + 1) * P, :], window[rb][:])

@@ -8,7 +8,8 @@ P = 128
 B, S, N = 1024, 512, 128
 K, H = 384, 512
 KB, HB, RB = K // P, H // P, B // P
-CHUNK = 512
+CHUNK = 256
+CHUNKS = B // CHUNK
 FLOPS = 2 * B * (K * H + H * 2 * N)
 
 
@@ -16,7 +17,7 @@ def tile_affine_coupling_layer_s_kernel(tc, base, xt, xid, cond, w1, b1, w3, off
     nc = tc.nc
     with (
         tc.tile_pool(name="held", bufs=1) as held,
-        tc.tile_pool(name="hidden", bufs=2) as hidden,
+        tc.tile_pool(name="hidden", bufs=3) as hidden,
         tc.tile_pool(name="work", bufs=3) as work,
         tc.psum_pool(name="psum_hid", bufs=4) as psum_hid,
         tc.psum_pool(name="psum_st", bufs=4) as psum_st,
@@ -44,7 +45,7 @@ def tile_affine_coupling_layer_s_kernel(tc, base, xt, xid, cond, w1, b1, w3, off
             queue = nc.sync if rb % 2 == 0 else nc.scalar
             queue.dma_start(window[rb][:], base[rb * P : (rb + 1) * P, :])
 
-        for c in range(B // CHUNK):
+        def first_layer(c):
             hid = hidden.tile([P, HB, CHUNK], BF16, name="hid")
             for hb in range(HB):
                 acc = psum_hid.tile([P, CHUNK], F32, name="acc")
@@ -57,7 +58,9 @@ def tile_affine_coupling_layer_s_kernel(tc, base, xt, xid, cond, w1, b1, w3, off
                         stop=(kb == KB - 1),
                     )
                 nc.scalar.activation(hid[:, hb, :], acc[:], ACT.Relu, bias=b1_sb[:, hb : hb + 1])
+            return hid
 
+        def coupling(c, hid):
             for i in range(CHUNK // P):
                 rb = c * (CHUNK // P) + i
                 st = psum_st.tile([P, 2 * N], F32, name="st")
@@ -77,3 +80,9 @@ def tile_affine_coupling_layer_s_kernel(tc, base, xt, xid, cond, w1, b1, w3, off
                 nc.vector.tensor_tensor(product[:], xt_sb[:, rb, :], scale[:], ALU.mult)
                 nc.vector.tensor_tensor(window[rb][:].indirect(offsets[:]), product[:], shift[:], ALU.add)
                 nc.sync.dma_start(out[rb * P : (rb + 1) * P, :], window[rb][:])
+
+        hid_of = {0: first_layer(0)}
+        for c in range(1, CHUNKS):
+            hid_of[c] = first_layer(c)
+            coupling(c - 1, hid_of[c - 1])
+        coupling(CHUNKS - 1, hid_of[CHUNKS - 1])

@@ -10,6 +10,7 @@ K, H = 384, 512
 KB, HB, RB = K // P, H // P, B // P
 CHUNK = 256
 CHUNKS = B // CHUNK
+BLOCKS = CHUNK // P
 FLOPS = 2 * B * (K * H + H * 2 * N)
 
 
@@ -17,72 +18,72 @@ def tile_affine_coupling_layer_s_kernel(tc, base, xt, xid, cond, w1, b1, w3, off
     nc = tc.nc
     with (
         tc.tile_pool(name="held", bufs=1) as held,
-        tc.tile_pool(name="hidden", bufs=3) as hidden,
         tc.tile_pool(name="work", bufs=3) as work,
         tc.psum_pool(name="psum_hid", bufs=4) as psum_hid,
         tc.psum_pool(name="psum_st", bufs=4) as psum_st,
     ):
-        offsets = held.tile([P, N // 16], U16, name="offsets")
-        nc.sync.dma_start(offsets[:], offs)
-
+        b1_sb = held.tile([P, HB], F32, name="b1_sb")
+        with nc.allow_non_contiguous_dma(reason="512 biases, one to a partition and block"):
+            nc.scalar.dma_start(b1_sb[:], b1.rearrange("(hb p) o -> p (hb o)", p=P))
         w1_sb = [held.tile([P, H], BF16, name=f"w1_sb{kb}") for kb in range(KB)]
         u_sb = [held.tile([P, B], BF16, name=f"u_sb{kb}") for kb in range(KB)]
         u_rows = [xid[0:P, :], xid[P : 2 * P, :], cond]
         for kb in range(KB):
             nc.sync.dma_start(w1_sb[kb][:], w1[kb * P : (kb + 1) * P, :])
-            nc.scalar.dma_start(u_sb[kb][:], u_rows[kb])
-
-        b1_sb = held.tile([P, HB], F32, name="b1_sb")
-        with nc.allow_non_contiguous_dma(reason="512 biases, one to a partition and block"):
-            nc.scalar.dma_start(b1_sb[:], b1.rearrange("(hb p) o -> p (hb o)", p=P))
+            nc.sync.dma_start(u_sb[kb][:], u_rows[kb])
+        offsets = held.tile([P, N // 16], U16, name="offsets")
+        nc.sync.dma_start(offsets[:], offs)
         w3_sb = held.tile([P, HB, 2 * N], BF16, name="w3_sb")
         nc.sync.dma_start(w3_sb[:], w3.rearrange("(hb p) j -> p hb j", p=P))
-        xt_sb = held.tile([P, RB, N], F32, name="xt_sb")
-        nc.scalar.dma_start(xt_sb[:], xt.rearrange("(rb p) j -> p rb j", p=P))
 
+        xt_sb = [held.tile([P, BLOCKS, N], F32, name=f"xt_sb{c}") for c in range(CHUNKS)]
         window = [held.tile([P, S], F32, name=f"window{rb}") for rb in range(RB)]
-        for rb in range(RB):
-            queue = nc.sync if rb % 2 == 0 else nc.scalar
-            queue.dma_start(window[rb][:], base[rb * P : (rb + 1) * P, :])
+        for c in range(CHUNKS):
+            nc.sync.dma_start(
+                xt_sb[c][:], xt[c * CHUNK : (c + 1) * CHUNK, :].rearrange("(i p) j -> p i j", p=P)
+            )
+            for rb in range(c * BLOCKS, (c + 1) * BLOCKS):
+                nc.sync.dma_start(window[rb][:], base[rb * P : (rb + 1) * P, :])
 
-        def first_layer(c):
-            hid = hidden.tile([P, HB, CHUNK], BF16, name="hid")
+        hid = [held.tile([P, HB, CHUNK], BF16, name=f"hid{c}") for c in range(CHUNKS)]
+
+        def first_layer(c, hb):
+            acc = psum_hid.tile([P, CHUNK], F32, name="acc")
+            for kb in range(KB):
+                nc.tensor.matmul(
+                    acc[:],
+                    w1_sb[kb][:, hb * P : (hb + 1) * P],
+                    u_sb[kb][:, c * CHUNK : (c + 1) * CHUNK],
+                    start=(kb == 0),
+                    stop=(kb == KB - 1),
+                )
+            if c == 0 and hb % 2 == 1:
+                nc.vector.tensor_scalar(hid[c][:, hb, :], acc[:], b1_sb[:, hb : hb + 1], 0.0, ALU.add, ALU.max)
+            else:
+                nc.scalar.activation(hid[c][:, hb, :], acc[:], ACT.Relu, bias=b1_sb[:, hb : hb + 1])
+
+        def coupling(c, i):
+            rb = c * BLOCKS + i
+            st = psum_st.tile([P, 2 * N], F32, name="st")
             for hb in range(HB):
-                acc = psum_hid.tile([P, CHUNK], F32, name="acc")
-                for kb in range(KB):
-                    nc.tensor.matmul(
-                        acc[:],
-                        w1_sb[kb][:, hb * P : (hb + 1) * P],
-                        u_sb[kb][:, c * CHUNK : (c + 1) * CHUNK],
-                        start=(kb == 0),
-                        stop=(kb == KB - 1),
-                    )
-                nc.scalar.activation(hid[:, hb, :], acc[:], ACT.Relu, bias=b1_sb[:, hb : hb + 1])
-            return hid
+                nc.tensor.matmul(
+                    st[:],
+                    hid[c][:, hb, i * P : (i + 1) * P],
+                    w3_sb[:, hb, :],
+                    start=(hb == 0),
+                    stop=(hb == HB - 1),
+                )
+            scale = work.tile([P, N], F32, name="scale")
+            nc.scalar.activation(scale[:], st[:, 0:N], ACT.Exp)
+            shift = work.tile([P, N], F32, name="shift")
+            nc.scalar.activation(shift[:], st[:, N : 2 * N], ACT.Copy)
+            product = work.tile([P, N], F32, name="product")
+            nc.vector.tensor_tensor(product[:], xt_sb[c][:, i, :], scale[:], ALU.mult)
+            nc.vector.tensor_tensor(window[rb][:].indirect(offsets[:]), product[:], shift[:], ALU.add)
+            nc.sync.dma_start(out[rb * P : (rb + 1) * P, :], window[rb][:])
 
-        def coupling(c, hid):
-            for i in range(CHUNK // P):
-                rb = c * (CHUNK // P) + i
-                st = psum_st.tile([P, 2 * N], F32, name="st")
-                for hb in range(HB):
-                    nc.tensor.matmul(
-                        st[:],
-                        hid[:, hb, i * P : (i + 1) * P],
-                        w3_sb[:, hb, :],
-                        start=(hb == 0),
-                        stop=(hb == HB - 1),
-                    )
-                scale = work.tile([P, N], F32, name="scale")
-                nc.scalar.activation(scale[:], st[:, 0:N], ACT.Exp)
-                shift = work.tile([P, N], F32, name="shift")
-                nc.scalar.activation(shift[:], st[:, N : 2 * N], ACT.Copy)
-                product = work.tile([P, N], F32, name="product")
-                nc.vector.tensor_tensor(product[:], xt_sb[:, rb, :], scale[:], ALU.mult)
-                nc.vector.tensor_tensor(window[rb][:].indirect(offsets[:]), product[:], shift[:], ALU.add)
-                nc.sync.dma_start(out[rb * P : (rb + 1) * P, :], window[rb][:])
-
-        hid_of = {0: first_layer(0)}
-        for c in range(1, CHUNKS):
-            hid_of[c] = first_layer(c)
-            coupling(c - 1, hid_of[c - 1])
-        coupling(CHUNKS - 1, hid_of[CHUNKS - 1])
+        for c in range(CHUNKS):
+            for hb in range(HB):
+                first_layer(c, hb)
+            for i in range(BLOCKS):
+                coupling(c, i)

@@ -11,6 +11,7 @@ KB, HB, RB = K // P, H // P, B // P
 CHUNK = 256
 CHUNKS = B // CHUNK
 BLOCKS = CHUNK // P
+WARM_MATMULS = 10
 FLOPS = 2 * B * (K * H + H * 2 * N)
 
 
@@ -44,6 +45,12 @@ def tile_affine_coupling_layer_s_kernel(tc, base, xt, xid, cond, w1, b1, w3, off
             )
             for rb in range(c * BLOCKS, (c + 1) * BLOCKS):
                 nc.sync.dma_start(window[rb][:], base[rb * P : (rb + 1) * P, :])
+
+        zeros = held.tile([P, 2 * N], BF16, name="zeros")
+        nc.vector.memset(zeros[:], 0.0)
+        warm = psum_st.tile([P, 2 * N], F32, name="warm", tag="st")
+        for w in range(WARM_MATMULS):
+            nc.tensor.matmul(warm[:], zeros[:, 0:P], zeros[:], start=True, stop=True)
 
         hid = [held.tile([P, HB, CHUNK], BF16, name=f"hid{c}") for c in range(CHUNKS)]
 

@@ -11,6 +11,8 @@ KB, HB, RB = K // P, H // P, B // P
 CHUNK = 256
 CHUNKS = B // CHUNK
 BLOCKS = CHUNK // P
+HALF = B // 2
+HALF_CHUNKS = HALF // CHUNK
 WARM_MATMULS = 10
 FLOPS = 2 * B * (K * H + H * 2 * N)
 
@@ -23,28 +25,34 @@ def tile_affine_coupling_layer_s_kernel(tc, base, xt, xid, cond, w1, b1, w3, off
         tc.psum_pool(name="psum_hid", bufs=4) as psum_hid,
         tc.psum_pool(name="psum_st", bufs=4) as psum_st,
     ):
-        b1_sb = held.tile([P, HB], F32, name="b1_sb")
-        with nc.allow_non_contiguous_dma(reason="512 biases, one to a partition and block"):
-            nc.scalar.dma_start(b1_sb[:], b1.rearrange("(hb p) o -> p (hb o)", p=P))
         w1_sb = [held.tile([P, H], BF16, name=f"w1_sb{kb}") for kb in range(KB)]
-        u_sb = [held.tile([P, B], BF16, name=f"u_sb{kb}") for kb in range(KB)]
+        u_sb = [[held.tile([P, HALF], BF16, name=f"u_sb{half}_{kb}") for kb in range(KB)] for half in range(2)]
         u_rows = [xid[0:P, :], xid[P : 2 * P, :], cond]
-        for kb in range(KB):
-            nc.sync.dma_start(w1_sb[kb][:], w1[kb * P : (kb + 1) * P, :])
-            nc.sync.dma_start(u_sb[kb][:], u_rows[kb])
-        offsets = held.tile([P, N // 16], U16, name="offsets")
-        nc.sync.dma_start(offsets[:], offs)
+        b1_sb = held.tile([P, HB], F32, name="b1_sb")
         w3_sb = held.tile([P, HB, 2 * N], BF16, name="w3_sb")
-        nc.sync.dma_start(w3_sb[:], w3.rearrange("(hb p) j -> p hb j", p=P))
-
+        offsets = held.tile([P, N // 16], U16, name="offsets")
         xt_sb = [held.tile([P, BLOCKS, N], F32, name=f"xt_sb{c}") for c in range(CHUNKS)]
         window = [held.tile([P, S], F32, name=f"window{rb}") for rb in range(RB)]
-        for c in range(CHUNKS):
+
+        def load_coupling_inputs(c):
             nc.sync.dma_start(
                 xt_sb[c][:], xt[c * CHUNK : (c + 1) * CHUNK, :].rearrange("(i p) j -> p i j", p=P)
             )
             for rb in range(c * BLOCKS, (c + 1) * BLOCKS):
                 nc.sync.dma_start(window[rb][:], base[rb * P : (rb + 1) * P, :])
+
+        for kb in range(KB):
+            nc.sync.dma_start(w1_sb[kb][:], w1[kb * P : (kb + 1) * P, :])
+            nc.sync.dma_start(u_sb[0][kb][:], u_rows[kb][:, 0:HALF])
+        with nc.allow_non_contiguous_dma(reason="512 biases, one to a partition and block"):
+            nc.sync.dma_start(b1_sb[:], b1.rearrange("(hb p) o -> p (hb o)", p=P))
+        nc.sync.dma_start(w3_sb[:], w3.rearrange("(hb p) j -> p hb j", p=P))
+        nc.sync.dma_start(offsets[:], offs)
+        load_coupling_inputs(0)
+        for kb in range(KB):
+            nc.sync.dma_start(u_sb[1][kb][:], u_rows[kb][:, HALF:B])
+        for c in range(1, CHUNKS):
+            load_coupling_inputs(c)
 
         zeros = held.tile([P, 2 * N], BF16, name="zeros")
         nc.vector.memset(zeros[:], 0.0)
@@ -60,7 +68,7 @@ def tile_affine_coupling_layer_s_kernel(tc, base, xt, xid, cond, w1, b1, w3, off
                 nc.tensor.matmul(
                     acc[:],
                     w1_sb[kb][:, hb * P : (hb + 1) * P],
-                    u_sb[kb][:, c * CHUNK : (c + 1) * CHUNK],
+                    u_sb[c // HALF_CHUNKS][kb][:, (c % HALF_CHUNKS) * CHUNK : (c % HALF_CHUNKS + 1) * CHUNK],
                     start=(kb == 0),
                     stop=(kb == KB - 1),
                 )

@@ -44,9 +44,8 @@ def tile_affine_coupling_layer_s_kernel(tc, base, xt, xid, cond, w1, b1, w3, off
         for kb in range(KB):
             nc.sync.dma_start(w1_sb[kb][:], w1[kb * P : (kb + 1) * P, :])
             nc.sync.dma_start(u_sb[0][kb][:], u_rows[kb][:, 0:HALF])
-        with nc.allow_non_contiguous_dma(reason="512 biases, one to a partition and block"):
-            nc.sync.dma_start(b1_sb[:], b1.rearrange("(hb p) o -> p (hb o)", p=P))
-        nc.sync.dma_start(w3_sb[:], w3.rearrange("(hb p) j -> p hb j", p=P))
+        nc.sync.dma_start(b1_sb[:], b1.rearrange("(p hb) o -> p (hb o)", hb=HB))
+        nc.sync.dma_start(w3_sb[:], w3.rearrange("(p hb) j -> p hb j", hb=HB))
         nc.sync.dma_start(offsets[:], offs)
         load_coupling_inputs(0)
         for kb in range(KB):
@@ -67,7 +66,7 @@ def tile_affine_coupling_layer_s_kernel(tc, base, xt, xid, cond, w1, b1, w3, off
             for kb in range(KB):
                 nc.tensor.matmul(
                     acc[:],
-                    w1_sb[kb][:, hb * P : (hb + 1) * P],
+                    w1_sb[kb][:].rearrange("k (p hb) -> k hb p", hb=HB)[:, hb, :],
                     u_sb[c // HALF_CHUNKS][kb][:, (c % HALF_CHUNKS) * CHUNK : (c % HALF_CHUNKS + 1) * CHUNK],
                     start=(kb == 0),
                     stop=(kb == KB - 1),

@@ -59,6 +59,9 @@ def tile_affine_coupling_layer_s_kernel(tc, base, xt, xid, cond, w1, b1, w3, off
         for w in range(WARM_MATMULS):
             nc.tensor.matmul(warm[:], zeros[:, 0:P], zeros[:], start=True, stop=True)
 
+        first_exp = held.tile([P, 1], F32, name="first_exp")
+        nc.scalar.activation(first_exp[:], zeros[:, 0:1], ACT.Exp)
+
         hid = [held.tile([P, HB, CHUNK], BF16, name=f"hid{c}") for c in range(CHUNKS)]
 
         def first_layer(c, hb):

@@ -74,10 +74,7 @@ def tile_affine_coupling_layer_s_kernel(tc, base, xt, xid, cond, w1, b1, w3, off
                     start=(kb == 0),
                     stop=(kb == KB - 1),
                 )
-            if c == 0 and hb % 2 == 1:
-                nc.vector.tensor_scalar(hid[c][:, hb, :], acc[:], b1_sb[:, hb : hb + 1], 0.0, ALU.add, ALU.max)
-            else:
-                nc.scalar.activation(hid[c][:, hb, :], acc[:], ACT.Relu, bias=b1_sb[:, hb : hb + 1])
+            nc.scalar.activation(hid[c][:, hb, :], acc[:], ACT.Relu, bias=b1_sb[:, hb : hb + 1])
 
         def coupling(c, i):
             rb = c * BLOCKS + i

@@ -13,7 +13,7 @@ CHUNKS = B // CHUNK
 BLOCKS = CHUNK // P
 HALF = B // 2
 HALF_CHUNKS = HALF // CHUNK
-WARM_MATMULS = 10
+WARM_MATMULS = 7
 FLOPS = 2 * B * (K * H + H * 2 * N)
 
 
@@ -64,17 +64,20 @@ def tile_affine_coupling_layer_s_kernel(tc, base, xt, xid, cond, w1, b1, w3, off
 
         hid = [held.tile([P, HB, CHUNK], BF16, name=f"hid{c}") for c in range(CHUNKS)]
 
-        def first_layer(c, hb):
-            acc = psum_hid.tile([P, CHUNK], F32, name="acc")
-            for kb in range(KB):
+        def first_layer(c, steps):
+            acc = {}
+            for hb, kb in steps:
+                if kb == 0:
+                    acc[hb] = psum_hid.tile([P, CHUNK], F32, name="acc")
                 nc.tensor.matmul(
-                    acc[:],
+                    acc[hb][:],
                     w1_sb[kb][:].rearrange("k (p hb) -> k hb p", hb=HB)[:, hb, :],
                     u_sb[c // HALF_CHUNKS][kb][:, (c % HALF_CHUNKS) * CHUNK : (c % HALF_CHUNKS + 1) * CHUNK],
                     start=(kb == 0),
                     stop=(kb == KB - 1),
                 )
-            nc.scalar.activation(hid[c][:, hb, :], acc[:], ACT.Relu, bias=b1_sb[:, hb : hb + 1])
+                if kb == KB - 1:
+                    nc.scalar.activation(hid[c][:, hb, :], acc[hb][:], ACT.Relu, bias=b1_sb[:, hb : hb + 1])
 
         def coupling(c, i):
             rb = c * BLOCKS + i
@@ -96,8 +99,9 @@ def tile_affine_coupling_layer_s_kernel(tc, base, xt, xid, cond, w1, b1, w3, off
             nc.vector.tensor_tensor(window[rb][:].indirect(offsets[:]), product[:], shift[:], ALU.add)
             nc.sync.dma_start(out[rb * P : (rb + 1) * P, :], window[rb][:])
 
+        by_feature_block = [(hb, kb) for kb in range(KB) for hb in range(HB)]
+        by_hidden_block = [(hb, kb) for hb in range(HB) for kb in range(KB)]
         for c in range(CHUNKS):
-            for hb in range(HB):
-                first_layer(c, hb)
+            first_layer(c, by_feature_block if c == 0 else by_hidden_block)
             for i in range(BLOCKS):
                 coupling(c, i)

@@ -22,8 +22,8 @@ def tile_affine_coupling_layer_s_kernel(tc, base, xt, xid, cond, w1, b1, w3, off
     with (
         tc.tile_pool(name="held", bufs=1) as held,
         tc.tile_pool(name="work", bufs=3) as work,
-        tc.psum_pool(name="psum_hid", bufs=4) as psum_hid,
-        tc.psum_pool(name="psum_st", bufs=4) as psum_st,
+        tc.psum_pool(name="psum_hid", bufs=5) as psum_hid,
+        tc.psum_pool(name="psum_st", bufs=3) as psum_st,
     ):
         w1_sb = [held.tile([P, H], BF16, name=f"w1_sb{kb}") for kb in range(KB)]
         u_sb = [[held.tile([P, HALF], BF16, name=f"u_sb{half}_{kb}") for kb in range(KB)] for half in range(2)]
@@ -46,11 +46,10 @@ def tile_affine_coupling_layer_s_kernel(tc, base, xt, xid, cond, w1, b1, w3, off
             nc.sync.dma_start(u_sb[0][kb][:], u_rows[kb][:, 0:HALF])
         nc.sync.dma_start(b1_sb[:], b1.rearrange("(p hb) o -> p (hb o)", hb=HB))
         nc.sync.dma_start(w3_sb[:], w3.rearrange("(p hb) j -> p hb j", hb=HB))
-        nc.sync.dma_start(offsets[:], offs)
-        load_coupling_inputs(0)
         for kb in range(KB):
             nc.sync.dma_start(u_sb[1][kb][:], u_rows[kb][:, HALF:B])
-        for c in range(1, CHUNKS):
+        nc.sync.dma_start(offsets[:], offs)
+        for c in range(CHUNKS):
             load_coupling_inputs(c)
 
         zeros = held.tile([P, 2 * N], BF16, name="zeros")

@@ -98,9 +98,11 @@ def tile_affine_coupling_layer_s_kernel(tc, base, xt, xid, cond, w1, b1, w3, off
             nc.vector.tensor_tensor(window[rb][:].indirect(offsets[:]), product[:], shift[:], ALU.add)
             nc.sync.dma_start(out[rb * P : (rb + 1) * P, :], window[rb][:])
 
-        by_feature_block = [(hb, kb) for kb in range(KB) for hb in range(HB)]
-        by_hidden_block = [(hb, kb) for hb in range(HB) for kb in range(KB)]
+        first_layer(0, [(hb, kb) for kb in range(KB) for hb in range(HB)])
         for c in range(CHUNKS):
-            first_layer(c, by_feature_block if c == 0 else by_hidden_block)
+            if c + 1 < CHUNKS:
+                first_layer(c + 1, [(0, kb) for kb in range(KB)])
             for i in range(BLOCKS):
                 coupling(c, i)
+            if c + 1 < CHUNKS:
+                first_layer(c + 1, [(hb, kb) for hb in range(1, HB) for kb in range(KB)])

@@ -76,33 +76,50 @@ def tile_affine_coupling_layer_s_kernel(tc, base, xt, xid, cond, w1, b1, w3, off
                     stop=(kb == KB - 1),
                 )
                 if kb == KB - 1:
-                    nc.scalar.activation(hid[c][:, hb, :], acc[hb][:], ACT.Relu, bias=b1_sb[:, hb : hb + 1])
+                    parts = BLOCKS if hb == HB - 1 else 1
+                    width = CHUNK // parts
+                    for part in range(parts):
+                        samples = slice(part * width, (part + 1) * width)
+                        nc.scalar.activation(
+                            hid[c][:, hb, samples], acc[hb][:, samples], ACT.Relu, bias=b1_sb[:, hb : hb + 1]
+                        )
 
-        def coupling(c, i):
-            rb = c * BLOCKS + i
-            st = psum_st.tile([P, 2 * N], F32, name="st")
+        def second_layer(c, i, columns):
+            st = psum_st.tile([P, columns.stop - columns.start], F32, name="st")
             for hb in range(HB):
                 nc.tensor.matmul(
                     st[:],
                     hid[c][:, hb, i * P : (i + 1) * P],
-                    w3_sb[:, hb, :],
+                    w3_sb[:, hb, columns],
                     start=(hb == 0),
                     stop=(hb == HB - 1),
                 )
+            return st
+
+        def coupling(c, i):
+            rb = c * BLOCKS + i
+            if rb < RB - 1:
+                st = second_layer(c, i, slice(0, 2 * N))
+                ls, t = st[:, 0:N], st[:, N : 2 * N]
+            else:
+                ls = second_layer(c, i, slice(0, N))[:]
             scale = work.tile([P, N], F32, name="scale")
-            nc.scalar.activation(scale[:], st[:, 0:N], ACT.Exp)
-            shift = work.tile([P, N], F32, name="shift")
-            nc.scalar.activation(shift[:], st[:, N : 2 * N], ACT.Copy)
+            nc.scalar.activation(scale[:], ls, ACT.Exp)
             product = work.tile([P, N], F32, name="product")
             nc.vector.tensor_tensor(product[:], xt_sb[c][:, i, :], scale[:], ALU.mult)
+            if rb == RB - 1:
+                t = second_layer(c, i, slice(N, 2 * N))[:]
+            shift = work.tile([P, N], F32, name="shift")
+            nc.scalar.activation(shift[:], t, ACT.Copy)
             nc.vector.tensor_tensor(window[rb][:].indirect(offsets[:]), product[:], shift[:], ALU.add)
             nc.sync.dma_start(out[rb * P : (rb + 1) * P, :], window[rb][:])
 
         first_layer(0, [(hb, kb) for kb in range(KB) for hb in range(HB)])
         for c in range(CHUNKS):
+            ahead = 1 if c + 1 < CHUNKS - 1 else 0
             if c + 1 < CHUNKS:
-                first_layer(c + 1, [(0, kb) for kb in range(KB)])
+                first_layer(c + 1, [(hb, kb) for hb in range(ahead) for kb in range(KB)])
             for i in range(BLOCKS):
                 coupling(c, i)
             if c + 1 < CHUNKS:
-                first_layer(c + 1, [(hb, kb) for hb in range(1, HB) for kb in range(KB)])
+                first_layer(c + 1, [(hb, kb) for hb in range(ahead, HB) for kb in range(KB)])

@@ -34,12 +34,15 @@ def tile_affine_coupling_layer_s_kernel(tc, base, xt, xid, cond, w1, b1, w3, off
         xt_sb = [held.tile([P, BLOCKS, N], F32, name=f"xt_sb{c}") for c in range(CHUNKS)]
         window = [held.tile([P, S], F32, name=f"window{rb}") for rb in range(RB)]
 
+        def block_rows(array, c, i):
+            return array[c * CHUNK : (c + 1) * CHUNK, :].rearrange("(p i) s -> p i s", i=BLOCKS)[:, i, :]
+
         def load_coupling_inputs(c):
             nc.sync.dma_start(
-                xt_sb[c][:], xt[c * CHUNK : (c + 1) * CHUNK, :].rearrange("(i p) j -> p i j", p=P)
+                xt_sb[c][:], xt[c * CHUNK : (c + 1) * CHUNK, :].rearrange("(p i) j -> p i j", i=BLOCKS)
             )
-            for rb in range(c * BLOCKS, (c + 1) * BLOCKS):
-                nc.sync.dma_start(window[rb][:], base[rb * P : (rb + 1) * P, :])
+            for i in range(BLOCKS):
+                nc.sync.dma_start(window[c * BLOCKS + i][:], block_rows(base, c, i))
 
         for kb in range(KB):
             nc.sync.dma_start(w1_sb[kb][:], w1[kb * P : (kb + 1) * P, :])
@@ -61,7 +64,7 @@ def tile_affine_coupling_layer_s_kernel(tc, base, xt, xid, cond, w1, b1, w3, off
         first_exp = held.tile([P, 1], F32, name="first_exp")
         nc.scalar.activation(first_exp[:], zeros[:, 0:1], ACT.Exp)
 
-        hid = [held.tile([P, HB, CHUNK], BF16, name=f"hid{c}") for c in range(CHUNKS)]
+        hid = [held.tile([P, HB, BLOCKS, P], BF16, name=f"hid{c}") for c in range(CHUNKS)]
 
         def first_layer(c, steps):
             acc = {}
@@ -76,12 +79,11 @@ def tile_affine_coupling_layer_s_kernel(tc, base, xt, xid, cond, w1, b1, w3, off
                     stop=(kb == KB - 1),
                 )
                 if kb == KB - 1:
-                    parts = BLOCKS if hb == HB - 1 else 1
-                    width = CHUNK // parts
-                    for part in range(parts):
-                        samples = slice(part * width, (part + 1) * width)
+                    by_block = acc[hb][:].rearrange("h (p i) -> h i p", i=BLOCKS)
+                    parts = [slice(i, i + 1) for i in range(BLOCKS)] if hb == HB - 1 else [slice(0, BLOCKS)]
+                    for part in parts:
                         nc.scalar.activation(
-                            hid[c][:, hb, samples], acc[hb][:, samples], ACT.Relu, bias=b1_sb[:, hb : hb + 1]
+                            hid[c][:, hb, part, :], by_block[:, part, :], ACT.Relu, bias=b1_sb[:, hb : hb + 1]
                         )
 
         def second_layer(c, i, columns):
@@ -89,7 +91,7 @@ def tile_affine_coupling_layer_s_kernel(tc, base, xt, xid, cond, w1, b1, w3, off
             for hb in range(HB):
                 nc.tensor.matmul(
                     st[:],
-                    hid[c][:, hb, i * P : (i + 1) * P],
+                    hid[c][:, hb, i, :],
                     w3_sb[:, hb, columns],
                     start=(hb == 0),
                     stop=(hb == HB - 1),
@@ -112,7 +114,7 @@ def tile_affine_coupling_layer_s_kernel(tc, base, xt, xid, cond, w1, b1, w3, off
             shift = work.tile([P, N], F32, name="shift")
             nc.scalar.activation(shift[:], t, ACT.Copy)
             nc.vector.tensor_tensor(window[rb][:].indirect(offsets[:]), product[:], shift[:], ALU.add)
-            nc.sync.dma_start(out[rb * P : (rb + 1) * P, :], window[rb][:])
+            nc.sync.dma_start(block_rows(out, c, i), window[rb][:])
 
         first_layer(0, [(hb, kb) for kb in range(KB) for hb in range(HB)])
         for c in range(CHUNKS):

@@ -13,7 +13,8 @@ CHUNKS = B // CHUNK
 BLOCKS = CHUNK // P
 HALF = B // 2
 HALF_CHUNKS = HALF // CHUNK
-WARM_MATMULS = 7
+XB = KB - 1
+WARM_MATMULS = 6
 FLOPS = 2 * B * (K * H + H * 2 * N)
 
 
@@ -25,9 +26,11 @@ def tile_affine_coupling_layer_s_kernel(tc, base, xt, xid, cond, w1, b1, w3, off
         tc.psum_pool(name="psum_hid", bufs=5) as psum_hid,
         tc.psum_pool(name="psum_st", bufs=3) as psum_st,
     ):
-        w1_sb = [held.tile([P, H], BF16, name=f"w1_sb{kb}") for kb in range(KB)]
-        u_sb = [[held.tile([P, HALF], BF16, name=f"u_sb{half}_{kb}") for kb in range(KB)] for half in range(2)]
-        u_rows = [xid[0:P, :], xid[P : 2 * P, :], cond]
+        w1_cond = held.tile([P, H], BF16, name="w1_cond")
+        w1_xid = held.tile([P, XB, H], BF16, name="w1_xid")
+        cond_early = [held.tile([P, CHUNK], BF16, name=f"cond_early{c}") for c in range(HALF_CHUNKS)]
+        cond_late = held.tile([P, B - HALF], BF16, name="cond_late")
+        xid_sb = [[held.tile([P, HALF], BF16, name=f"xid_sb{half}_{xb}") for xb in range(XB)] for half in range(2)]
         b1_sb = held.tile([P, HB], F32, name="b1_sb")
         w3_sb = held.tile([P, HB, 2 * N], BF16, name="w3_sb")
         offsets = held.tile([P, N // 16], U16, name="offsets")
@@ -44,13 +47,20 @@ def tile_affine_coupling_layer_s_kernel(tc, base, xt, xid, cond, w1, b1, w3, off
             for i in range(BLOCKS):
                 nc.sync.dma_start(window[c * BLOCKS + i][:], block_rows(base, c, i))
 
-        for kb in range(KB):
-            nc.sync.dma_start(w1_sb[kb][:], w1[kb * P : (kb + 1) * P, :])
-            nc.sync.dma_start(u_sb[0][kb][:], u_rows[kb][:, 0:HALF])
+        def load_xid(half):
+            for xb in range(XB):
+                rows = xid.rearrange("(p xb) r -> p xb r", xb=XB)[:, xb, :]
+                nc.sync.dma_start(xid_sb[half][xb][:], rows[:, half * HALF : (half + 1) * HALF])
+
+        nc.sync.dma_start(w1_cond[:], w1[XB * P : K, :])
+        nc.sync.dma_start(cond_early[0][:], cond[:, 0:CHUNK])
+        nc.sync.dma_start(w1_xid[:], w1[0 : XB * P, :].rearrange("(p xb) h -> p xb h", xb=XB))
+        load_xid(0)
         nc.sync.dma_start(b1_sb[:], b1.rearrange("(p hb) o -> p (hb o)", hb=HB))
+        nc.sync.dma_start(cond_early[1][:], cond[:, CHUNK:HALF])
         nc.sync.dma_start(w3_sb[:], w3.rearrange("(p hb) j -> p hb j", hb=HB))
-        for kb in range(KB):
-            nc.sync.dma_start(u_sb[1][kb][:], u_rows[kb][:, HALF:B])
+        nc.sync.dma_start(cond_late[:], cond[:, HALF:B])
+        load_xid(1)
         nc.sync.dma_start(offsets[:], offs)
         for c in range(CHUNKS):
             load_coupling_inputs(c)
@@ -66,6 +76,17 @@ def tile_affine_coupling_layer_s_kernel(tc, base, xt, xid, cond, w1, b1, w3, off
 
         hid = [held.tile([P, HB, BLOCKS, P], BF16, name=f"hid{c}") for c in range(CHUNKS)]
 
+        def w1_block(hb, kb):
+            rows = w1_cond[:] if kb == 0 else w1_xid[:, kb - 1, :]
+            return rows.rearrange("k (p hb) -> k hb p", hb=HB)[:, hb, :]
+
+        def u_columns(c, kb):
+            half = c // HALF_CHUNKS
+            columns = slice((c % HALF_CHUNKS) * CHUNK, (c % HALF_CHUNKS + 1) * CHUNK)
+            if kb > 0:
+                return xid_sb[half][kb - 1][:, columns]
+            return cond_early[c][:] if half == 0 else cond_late[:, columns]
+
         def first_layer(c, steps):
             acc = {}
             for hb, kb in steps:
@@ -73,8 +94,8 @@ def tile_affine_coupling_layer_s_kernel(tc, base, xt, xid, cond, w1, b1, w3, off
                     acc[hb] = psum_hid.tile([P, CHUNK], F32, name="acc")
                 nc.tensor.matmul(
                     acc[hb][:],
-                    w1_sb[kb][:].rearrange("k (p hb) -> k hb p", hb=HB)[:, hb, :],
-                    u_sb[c // HALF_CHUNKS][kb][:, (c % HALF_CHUNKS) * CHUNK : (c % HALF_CHUNKS + 1) * CHUNK],
+                    w1_block(hb, kb),
+                    u_columns(c, kb),
                     start=(kb == 0),
                     stop=(kb == KB - 1),
                 )
@@ -98,30 +119,38 @@ def tile_affine_coupling_layer_s_kernel(tc, base, xt, xid, cond, w1, b1, w3, off
                 )
             return st
 
-        def coupling(c, i):
-            rb = c * BLOCKS + i
-            if rb < RB - 1:
-                st = second_layer(c, i, slice(0, 2 * N))
-                ls, t = st[:, 0:N], st[:, N : 2 * N]
-            else:
-                ls = second_layer(c, i, slice(0, N))[:]
+        def scale_by(c, i, ls):
             scale = work.tile([P, N], F32, name="scale")
             nc.scalar.activation(scale[:], ls, ACT.Exp)
             product = work.tile([P, N], F32, name="product")
             nc.vector.tensor_tensor(product[:], xt_sb[c][:, i, :], scale[:], ALU.mult)
-            if rb == RB - 1:
-                t = second_layer(c, i, slice(N, 2 * N))[:]
+            return product
+
+        def place(c, i, product, t):
             shift = work.tile([P, N], F32, name="shift")
             nc.scalar.activation(shift[:], t, ACT.Copy)
-            nc.vector.tensor_tensor(window[rb][:].indirect(offsets[:]), product[:], shift[:], ALU.add)
-            nc.sync.dma_start(block_rows(out, c, i), window[rb][:])
+            rows = window[c * BLOCKS + i]
+            nc.vector.tensor_tensor(rows[:].indirect(offsets[:]), product[:], shift[:], ALU.add)
+            nc.sync.dma_start(block_rows(out, c, i), rows[:])
+
+        def coupling(c, i):
+            st = second_layer(c, i, slice(0, 2 * N))
+            place(c, i, scale_by(c, i, st[:, 0:N]), st[:, N : 2 * N])
+
+        def last_couplings(c):
+            st = second_layer(c, 0, slice(0, 2 * N))
+            first = scale_by(c, 0, st[:, 0:N])
+            second = scale_by(c, 1, second_layer(c, 1, slice(0, N))[:])
+            place(c, 0, first, st[:, N : 2 * N])
+            place(c, 1, second, second_layer(c, 1, slice(N, 2 * N))[:])
 
         first_layer(0, [(hb, kb) for kb in range(KB) for hb in range(HB)])
         for c in range(CHUNKS):
             ahead = 1 if c + 1 < CHUNKS - 1 else 0
             if c + 1 < CHUNKS:
                 first_layer(c + 1, [(hb, kb) for hb in range(ahead) for kb in range(KB)])
-            for i in range(BLOCKS):
-                coupling(c, i)
-            if c + 1 < CHUNKS:
+                for i in range(BLOCKS):
+                    coupling(c, i)
                 first_layer(c + 1, [(hb, kb) for hb in range(ahead, HB) for kb in range(KB)])
+            else:
+                last_couplings(c)

import concourse.mybir as mybir

F32, BF16, U16 = mybir.dt.float32, mybir.dt.bfloat16, mybir.dt.uint16
ACT = mybir.ActivationFunctionType
ALU = mybir.AluOpType

P = 128
B, S, N = 1024, 512, 128
K, H = 384, 512
KB, HB, RB = K // P, H // P, B // P
CHUNK = 256
CHUNKS = B // CHUNK
BLOCKS = CHUNK // P
HALF = B // 2
HALF_CHUNKS = HALF // CHUNK
XB = KB - 1
WARM_MATMULS = 6
FLOPS = 2 * B * (K * H + H * 2 * N)


def tile_affine_coupling_layer_s_kernel(tc, base, xt, xid, cond, w1, b1, w3, offs, out):
    nc = tc.nc
    with (
        tc.tile_pool(name="held", bufs=1) as held,
        tc.tile_pool(name="work", bufs=3) as work,
        tc.psum_pool(name="psum_hid", bufs=5) as psum_hid,
        tc.psum_pool(name="psum_st", bufs=3) as psum_st,
    ):
        w1_cond = held.tile([P, H], BF16, name="w1_cond")
        w1_xid = held.tile([P, XB, H], BF16, name="w1_xid")
        cond_early = [held.tile([P, CHUNK], BF16, name=f"cond_early{c}") for c in range(HALF_CHUNKS)]
        cond_late = held.tile([P, B - HALF], BF16, name="cond_late")
        xid_sb = [[held.tile([P, HALF], BF16, name=f"xid_sb{half}_{xb}") for xb in range(XB)] for half in range(2)]
        b1_sb = held.tile([P, HB], F32, name="b1_sb")
        w3_sb = held.tile([P, HB, 2 * N], BF16, name="w3_sb")
        offsets = held.tile([P, N // 16], U16, name="offsets")
        xt_sb = [held.tile([P, BLOCKS, N], F32, name=f"xt_sb{c}") for c in range(CHUNKS)]
        window = [held.tile([P, S], F32, name=f"window{rb}") for rb in range(RB)]

        def block_rows(array, c, i):
            return array[c * CHUNK : (c + 1) * CHUNK, :].rearrange("(p i) s -> p i s", i=BLOCKS)[:, i, :]

        def load_coupling_inputs(c):
            nc.sync.dma_start(
                xt_sb[c][:], xt[c * CHUNK : (c + 1) * CHUNK, :].rearrange("(p i) j -> p i j", i=BLOCKS)
            )
            for i in range(BLOCKS):
                nc.sync.dma_start(window[c * BLOCKS + i][:], block_rows(base, c, i))

        def load_xid(half):
            for xb in range(XB):
                rows = xid.rearrange("(p xb) r -> p xb r", xb=XB)[:, xb, :]
                nc.sync.dma_start(xid_sb[half][xb][:], rows[:, half * HALF : (half + 1) * HALF])

        nc.sync.dma_start(w1_cond[:], w1[XB * P : K, :])
        nc.sync.dma_start(cond_early[0][:], cond[:, 0:CHUNK])
        nc.sync.dma_start(w1_xid[:], w1[0 : XB * P, :].rearrange("(p xb) h -> p xb h", xb=XB))
        load_xid(0)
        nc.sync.dma_start(b1_sb[:], b1.rearrange("(p hb) o -> p (hb o)", hb=HB))
        nc.sync.dma_start(cond_early[1][:], cond[:, CHUNK:HALF])
        nc.sync.dma_start(w3_sb[:], w3.rearrange("(p hb) j -> p hb j", hb=HB))
        nc.sync.dma_start(cond_late[:], cond[:, HALF:B])
        load_xid(1)
        nc.sync.dma_start(offsets[:], offs)
        for c in range(CHUNKS):
            load_coupling_inputs(c)

        zeros = held.tile([P, 2 * N], BF16, name="zeros")
        nc.vector.memset(zeros[:], 0.0)
        warm = psum_st.tile([P, 2 * N], F32, name="warm", tag="st")
        for w in range(WARM_MATMULS):
            nc.tensor.matmul(warm[:], zeros[:, 0:P], zeros[:], start=True, stop=True)

        first_exp = held.tile([P, 1], F32, name="first_exp")
        nc.scalar.activation(first_exp[:], zeros[:, 0:1], ACT.Exp)

        hid = [held.tile([P, HB, BLOCKS, P], BF16, name=f"hid{c}") for c in range(CHUNKS)]

        def w1_block(hb, kb):
            rows = w1_cond[:] if kb == 0 else w1_xid[:, kb - 1, :]
            return rows.rearrange("k (p hb) -> k hb p", hb=HB)[:, hb, :]

        def u_columns(c, kb):
            half = c // HALF_CHUNKS
            columns = slice((c % HALF_CHUNKS) * CHUNK, (c % HALF_CHUNKS + 1) * CHUNK)
            if kb > 0:
                return xid_sb[half][kb - 1][:, columns]
            return cond_early[c][:] if half == 0 else cond_late[:, columns]

        def first_layer(c, steps):
            acc = {}
            for hb, kb in steps:
                if kb == 0:
                    acc[hb] = psum_hid.tile([P, CHUNK], F32, name="acc")
                nc.tensor.matmul(
                    acc[hb][:],
                    w1_block(hb, kb),
                    u_columns(c, kb),
                    start=(kb == 0),
                    stop=(kb == KB - 1),
                )
                if kb == KB - 1:
                    by_block = acc[hb][:].rearrange("h (p i) -> h i p", i=BLOCKS)
                    parts = [slice(i, i + 1) for i in range(BLOCKS)] if hb == HB - 1 else [slice(0, BLOCKS)]
                    for part in parts:
                        nc.scalar.activation(
                            hid[c][:, hb, part, :], by_block[:, part, :], ACT.Relu, bias=b1_sb[:, hb : hb + 1]
                        )

        def second_layer(c, i, columns):
            st = psum_st.tile([P, columns.stop - columns.start], F32, name="st")
            for hb in range(HB):
                nc.tensor.matmul(
                    st[:],
                    hid[c][:, hb, i, :],
                    w3_sb[:, hb, columns],
                    start=(hb == 0),
                    stop=(hb == HB - 1),
                )
            return st

        def scale_by(c, i, ls):
            scale = work.tile([P, N], F32, name="scale")
            nc.scalar.activation(scale[:], ls, ACT.Exp)
            product = work.tile([P, N], F32, name="product")
            nc.vector.tensor_tensor(product[:], xt_sb[c][:, i, :], scale[:], ALU.mult)
            return product

        def place(c, i, product, t):
            shift = work.tile([P, N], F32, name="shift")
            nc.scalar.activation(shift[:], t, ACT.Copy)
            rows = window[c * BLOCKS + i]
            nc.vector.tensor_tensor(rows[:].indirect(offsets[:]), product[:], shift[:], ALU.add)
            nc.sync.dma_start(block_rows(out, c, i), rows[:])

        def coupling(c, i):
            st = second_layer(c, i, slice(0, 2 * N))
            place(c, i, scale_by(c, i, st[:, 0:N]), st[:, N : 2 * N])

        def last_couplings(c):
            st = second_layer(c, 0, slice(0, 2 * N))
            first = scale_by(c, 0, st[:, 0:N])
            second = scale_by(c, 1, second_layer(c, 1, slice(0, N))[:])
            place(c, 0, first, st[:, N : 2 * N])
            place(c, 1, second, second_layer(c, 1, slice(N, 2 * N))[:])

        first_layer(0, [(hb, kb) for kb in range(KB) for hb in range(HB)])
        for c in range(CHUNKS):
            ahead = 1 if c + 1 < CHUNKS - 1 else 0
            if c + 1 < CHUNKS:
                first_layer(c + 1, [(hb, kb) for hb in range(ahead) for kb in range(KB)])
                for i in range(BLOCKS):
                    coupling(c, i)
                first_layer(c + 1, [(hb, kb) for hb in range(ahead, HB) for kb in range(KB)])
            else:
                last_couplings(c)
